import numpy as np
import ml_dtypes


def mxq(x, axis, fmt="e4m3"):
    dtype, down = {"e4m3": (ml_dtypes.float8_e4m3fn, 7), "e5m2": (ml_dtypes.float8_e5m2, 14)}[fmt]
    v = np.moveaxis(np.asarray(x, np.float32).astype(ml_dtypes.bfloat16).astype(np.float64), axis, -1)
    blocks = v.reshape(v.shape[:-1] + (-1, 32))
    amax = np.abs(blocks).max(-1, keepdims=True)
    byte = np.maximum(np.where(amax > 0, np.frexp(amax)[1] - 1 + 127, 0) - down, 1)
    scale = np.exp2(byte - 127.0)
    codes = (blocks / scale).astype(np.float32).astype(dtype).astype(np.float64)
    return np.moveaxis((codes * scale).reshape(v.shape), -1, axis)


WIDE = False


def mx_kscale(k):
    if not WIDE:
        return np.ones(k)
    levels = np.array([10, -10, 5, -5, 0])
    a = np.random.permutation(np.resize(levels, k // 512 * 4)).reshape(k // 512, 4)
    idx = np.arange(k)
    return np.exp2(a[idx // 512, idx % 128 // 32])


BF16 = ml_dtypes.bfloat16


def bf(x):
    return np.asarray(x, np.float32).astype(BF16)


def f64(x):
    return np.asarray(x).astype(np.float64)


B, C, K, H, W = 32, 256, 128, 32, 32
N = H * W


def setup_inputs():
    s = mx_kscale(N)
    feats = np.random.standard_normal((B, C, N)) * 4.0 * s.mean() / s
    probs = np.random.standard_normal((B, K, N)) * 2.0 + np.log(s)
    return {"feats": bf(feats.reshape(B, C, H, W)), "probs": bf(probs.reshape(B, K, H, W))}


def reference(feats, probs):
    x = f64(feats).reshape(B, C, N)
    l = f64(probs).reshape(B, K, N)
    e = np.exp(l - l.max(2, keepdims=True))
    ctx = (mxq(e, 2, "e4m3") @ mxq(x, 2, "e4m3").transpose(0, 2, 1)) / e.sum(2, keepdims=True)
    return ctx.transpose(0, 2, 1)[..., None]

@@ -1,0 +1,227 @@
+from contextlib import ExitStack
+
+import concourse.mybir as mybir
+from concourse.masks import make_identity
+
+BF16 = mybir.dt.bfloat16
+F32 = mybir.dt.float32
+U32 = mybir.dt.uint32
+U8 = mybir.dt.uint8
+FP8X4 = mybir.dt.float8_e4m3fn_x4
+ACT = mybir.ActivationFunctionType
+ALU = mybir.AluOpType
+AX = mybir.AxisListType
+
+B = 32
+C = 256
+K = 128
+N = 1024
+P = 128
+NP = B // 2
+FLOPS = 2 * B * K * C * N
+
+PIN = False
+DX = 1
+N_SCALAR_BANKS = 1
+
+
+def tile_spatialgather_module_t_kernel(tc, feats, probs, out):
+    nc = tc.nc
+    with ExitStack() as ctx:
+        const = ctx.enter_context(tc.tile_pool(name="const", bufs=1))
+        lpool = ctx.enter_context(tc.tile_pool(name="lpool", bufs=8))
+        xpool = ctx.enter_context(tc.tile_pool(name="xpool", bufs=8))
+        tree = ctx.enter_context(tc.tile_pool(name="tree", bufs=2))
+        small = ctx.enter_context(tc.tile_pool(name="small", bufs=8))
+        epool = ctx.enter_context(tc.tile_pool(name="epool", bufs=4))
+        gpool = ctx.enter_context(tc.tile_pool(name="gpool", bufs=3))
+        qpool = ctx.enter_context(tc.tile_pool(name="qpool", bufs=DX + 3))
+        opool = ctx.enter_context(tc.tile_pool(name="opool", bufs=3))
+        psum = ctx.enter_context(tc.psum_pool(name="psum", bufs=1))
+
+        ident_bf = const.tile([P, P], BF16, name="ident_bf")
+        make_identity(nc, ident_bf[:])
+        ident_f = const.tile([P, P], F32, name="ident_f")
+        make_identity(nc, ident_f[:])
+
+        l_sb, x_sb, negmax, rowsum, e_sb = {}, {}, {}, {}, {}
+        ge, gx, eq, es, xq, xs, rinv, rec, rt_ps, ctx_ps = {}, {}, {}, {}, {}, {}, {}, {}, {}, {}
+
+        def load_l(s):
+            t = lpool.tile([P, 2, N], BF16, name="l_sb")
+            nc.sync.dma_start(out=t[:], in_=probs[2 * s : 2 * s + 2].rearrange("b k y x -> k b (y x)"))
+            l_sb[s] = t
+
+        def load_x(s):
+            t = xpool.tile([P, 2, 2 * N], BF16, name="x_sb")
+            nc.sync.dma_start(
+                out=t[:], in_=feats[2 * s : 2 * s + 2].rearrange("b (p h) y x -> p b (h y x)", h=2)
+            )
+            x_sb[s] = t
+
+        def row_max(s):
+            src = l_sb[s]
+            for width in (512, 256, 128, 64):
+                dst = tree.tile([P, 2, width], BF16, name="m%d" % width)
+                nc.vector.tensor_tensor(
+                    out=dst[:], in0=src[:, :, 0:width], in1=src[:, :, width : 2 * width], op=ALU.max
+                )
+                src = dst
+            mx = small.tile([P, 2], F32, name="mx")
+            nc.vector.tensor_reduce(out=mx[:], in_=src[:], axis=AX.X, op=ALU.max)
+            nm = small.tile([P, 2], F32, name="nm")
+            nc.vector.tensor_scalar_mul(out=nm[:], in0=mx[:], scalar1=-1.0)
+            negmax[s] = nm
+
+        def exps(s):
+            rs = small.tile([P, 2], F32, name="rs")
+            rowsum[s] = rs
+            for j in range(2):
+                e = epool.tile([P, N], BF16, name="e_sb")
+                nc.scalar.activation(
+                    out=e[:].rearrange("k (a e p) -> k a e p", a=4, e=2),
+                    in_=l_sb[s][:, j, :].rearrange("k (a p e) -> k a e p", a=4, e=2),
+                    func=ACT.Exp,
+                    bias=negmax[s][:, j : j + 1],
+                    scale=1.0,
+                    accum_out=rs[:, j : j + 1],
+                )
+                e_sb[(s, j)] = e
+
+        et_ps = {}
+
+        def te(s):
+            for j in range(2):
+                et = psum.tile([P, 8, P], BF16, name="et", bufs=2)
+                for ch in range(8):
+                    nc.tensor.transpose(et[:, ch, :], e_sb[(s, j)][:, ch * P : (ch + 1) * P], ident_bf[:])
+                et_ps[(s, j)] = et
+
+        def ce(s):
+            g = gpool.tile([P, 2 * N], BF16, name="ge", align_bytes=64)
+            ge[s] = g
+            gv = g[:].rearrange("p (i g k t) -> p i g k t", i=2, g=2, t=4)
+            for j in range(2):
+                nc.scalar.copy(out=gv[:, j], in_=et_ps[(s, j)][:].rearrange("p (g t) k -> p g k t", t=4))
+
+        xt_ps = {}
+
+        def tx(s):
+            for j in range(2):
+                xw = x_sb[s][:, j, :].bitcast(F32)
+                for g in range(2):
+                    xt = psum.tile([P, 4, P], F32, name="xt", bufs=4)
+                    for h in range(2):
+                        for u in range(2):
+                            w0 = 512 * h + 256 * g + 128 * u
+                            nc.tensor.transpose(xt[:, 2 * h + u, :], xw[:, w0 : w0 + P], ident_f[:])
+                    xt_ps[(s, j, g)] = xt
+
+        def cx(s, banks, on_scalar):
+            if s not in gx:
+                gx[s] = gpool.tile([P, 4 * N], BF16, name="gx", align_bytes=64)
+            gw = gx[s][:].bitcast(F32).rearrange("p (i g h c u) -> p i g h c u", i=2, g=2, h=2, u=2)
+            for b in banks:
+                j, g = b // 2, b % 2
+                src = xt_ps[(s, j, g)][:].rearrange("p (h u) c -> p h c u", u=2)
+                if on_scalar:
+                    nc.scalar.copy(out=gw[:, j, g], in_=src)
+                else:
+                    nc.vector.tensor_copy(out=gw[:, j, g], in_=src)
+
+        def qe(s):
+            eq[s] = qpool.tile([P, N // 2], U32, name="eq", align_bytes=64)
+            es[s] = qpool.tile([P, N // 2], U8, name="es", align_bytes=64)
+            nc.vector.quantize_mx(out=eq[s][:].bitcast(FP8X4), scales=es[s][:], in_=ge[s][:])
+
+        def qx(s):
+            xq[s] = qpool.tile([P, N], U32, name="xq", align_bytes=64)
+            xs[s] = qpool.tile([P, N], U8, name="xs", align_bytes=64)
+            nc.vector.quantize_mx(out=xq[s][:].bitcast(FP8X4), scales=xs[s][:], in_=gx[s][:])
+
+        def recip(s):
+            rec[s] = small.tile([P, 2], F32, name="rec")
+            nc.vector.reciprocal(out=rec[s][:], in_=rowsum[s][:])
+
+        def rt_t(s):
+            rt = psum.tile([P, 2, P], F32, name="rt", bufs=1)
+            for j in range(2):
+                nc.tensor.transpose(rt[:, j, :], rec[s][:, j : j + 1].to_broadcast([P, P]), ident_f[:])
+            rt_ps[s] = rt
+
+        def rt_copy(s):
+            rinv[s] = opool.tile([P, 2, P], F32, name="rinv")
+            nc.scalar.copy(out=rinv[s][:], in_=rt_ps[s][:])
+
+        def mm(s):
+            acc = psum.tile([P, 4 * P], F32, name="acc", bufs=1)
+            ctx_ps[s] = acc
+            for j in range(2):
+                for h in range(2):
+                    for g in range(2):
+                        xo = ((j * 2 + g) * 2 + h) * P
+                        eo = (j * 2 + g) * P
+                        nc.tensor.matmul_mx(
+                            out=acc[:, (j * 2 + h) * P : (j * 2 + h + 1) * P],
+                            lhsT=xq[s][:, xo : xo + P].bitcast(FP8X4),
+                            lhsT_scale=xs[s][:, xo : xo + P],
+                            rhs=eq[s][:, eo : eo + P].bitcast(FP8X4),
+                            rhs_scale=es[s][:, eo : eo + P],
+                            start=(g == 0),
+                            stop=(g == 1),
+                        )
+
+        def fin(s):
+            o = opool.tile([P, 2, 2, P], F32, name="o_sb")
+            nc.vector.tensor_tensor(
+                out=o[:],
+                in0=ctx_ps[s][:].rearrange("p (i h k) -> p i h k", i=2, h=2),
+                in1=rinv[s][:].unsqueeze(2).to_broadcast([P, 2, 2, P]),
+                op=ALU.mult,
+            )
+            nc.gpsimd.dma_start(
+                out=out[2 * s : 2 * s + 2].rearrange("b (p h) k o -> p b (h k o)", h=2),
+                in_=o[:].rearrange("p i h k -> p i (h k)"),
+            )
+
+        def ok(s):
+            return 0 <= s < NP
+
+        if PIN:
+            ctx.enter_context(tc.manual_schedule())
+
+        LOOK = 5
+        for s in range(LOOK):
+            load_l(s)
+            load_x(s)
+        for s in range(-3, NP + 1):
+            if ok(s + 3 + LOOK):
+                load_l(s + 3 + LOOK)
+                load_x(s + 3 + LOOK)
+            if ok(s):
+                recip(s)
+            if ok(s + DX):
+                tx(s + DX)
+            if ok(s + 1):
+                te(s + 1)
+            if ok(s):
+                rt_t(s)
+            if ok(s - 1):
+                mm(s - 1)
+            if ok(s):
+                qe(s)
+            if ok(s + 1):
+                ce(s + 1)
+            if ok(s + DX):
+                cx(s + DX, range(N_SCALAR_BANKS, 4), False)
+                cx(s + DX, range(0, N_SCALAR_BANKS), True)
+            if ok(s + 3):
+                row_max(s + 3)
+            if ok(s + 2):
+                exps(s + 2)
+            if ok(s + DX):
+                qx(s + DX)
+            if ok(s):
+                rt_copy(s)
+            if ok(s - 1):
+                fin(s - 1)

@@ -20,8 +20,8 @@ P = 128
 NP = B // 2
 FLOPS = 2 * B * K * C * N
 
-PIN = False
-DX = 1
+PIN = True
+DX = 2
 N_SCALAR_BANKS = 1
 
 
@@ -33,7 +33,7 @@ def tile_spatialgather_module_t_kernel(tc, feats, probs, out):
         xpool = ctx.enter_context(tc.tile_pool(name="xpool", bufs=8))
         tree = ctx.enter_context(tc.tile_pool(name="tree", bufs=2))
         small = ctx.enter_context(tc.tile_pool(name="small", bufs=8))
-        epool = ctx.enter_context(tc.tile_pool(name="epool", bufs=4))
+        epool = ctx.enter_context(tc.tile_pool(name="epool", bufs=8))
         gpool = ctx.enter_context(tc.tile_pool(name="gpool", bufs=3))
         qpool = ctx.enter_context(tc.tile_pool(name="qpool", bufs=DX + 3))
         opool = ctx.enter_context(tc.tile_pool(name="opool", bufs=3))
@@ -60,17 +60,18 @@ def tile_spatialgather_module_t_kernel(tc, feats, probs, out):
             x_sb[s] = t
 
         def row_max(s):
-            src = l_sb[s]
-            for width in (512, 256, 128, 64):
-                dst = tree.tile([P, 2, width], BF16, name="m%d" % width)
-                nc.vector.tensor_tensor(
-                    out=dst[:], in0=src[:, :, 0:width], in1=src[:, :, width : 2 * width], op=ALU.max
-                )
-                src = dst
-            mx = small.tile([P, 2], F32, name="mx")
-            nc.vector.tensor_reduce(out=mx[:], in_=src[:], axis=AX.X, op=ALU.max)
             nm = small.tile([P, 2], F32, name="nm")
-            nc.vector.tensor_scalar_mul(out=nm[:], in0=mx[:], scalar1=-1.0)
+            for j in range(2):
+                junk = tree.tile([P, N], BF16, name="junk")
+                nc.vector.tensor_scalar(
+                    out=junk[:],
+                    in0=l_sb[s][:, j, :],
+                    scalar1=-1.0,
+                    scalar2=None,
+                    op0=ALU.mult,
+                    op1=ALU.min,
+                    accum_out=nm[:, j : j + 1],
+                )
             negmax[s] = nm
 
         def exps(s):
@@ -179,7 +180,8 @@ def tile_spatialgather_module_t_kernel(tc, feats, probs, out):
                 in1=rinv[s][:].unsqueeze(2).to_broadcast([P, 2, 2, P]),
                 op=ALU.mult,
             )
-            nc.gpsimd.dma_start(
+            queue = nc.sync if s >= NP - 4 else nc.gpsimd
+            queue.dma_start(
                 out=out[2 * s : 2 * s + 2].rearrange("b (p h) k o -> p b (h k o)", h=2),
                 in_=o[:].rearrange("p i h k -> p i (h k)"),
             )
@@ -194,31 +196,32 @@ def tile_spatialgather_module_t_kernel(tc, feats, probs, out):
         for s in range(LOOK):
             load_l(s)
             load_x(s)
-        for s in range(-3, NP + 1):
-            if ok(s + 3 + LOOK):
-                load_l(s + 3 + LOOK)
-                load_x(s + 3 + LOOK)
+        for s in range(-4, NP + 1):
+            if ok(s + 4 + LOOK):
+                load_l(s + 4 + LOOK)
+                load_x(s + 4 + LOOK)
             if ok(s):
                 recip(s)
-            if ok(s + DX):
-                tx(s + DX)
             if ok(s + 1):
                 te(s + 1)
+            if ok(s + DX):
+                tx(s + DX)
             if ok(s):
                 rt_t(s)
             if ok(s - 1):
                 mm(s - 1)
             if ok(s):
                 qe(s)
+            if ok(s + DX):
+                cx(s + DX, range(0, N_SCALAR_BANKS), True)
             if ok(s + 1):
                 ce(s + 1)
             if ok(s + DX):
                 cx(s + DX, range(N_SCALAR_BANKS, 4), False)
-                cx(s + DX, range(0, N_SCALAR_BANKS), True)
+            if ok(s + 4):
+                row_max(s + 4)
             if ok(s + 3):
-                row_max(s + 3)
-            if ok(s + 2):
-                exps(s + 2)
+                exps(s + 3)
             if ok(s + DX):
                 qx(s + DX)
             if ok(s):

@@ -147,7 +147,13 @@ def tile_spatialgather_module_t_kernel(tc, feats, probs, out):
         def rt_t(s):
             rt = psum.tile([P, 2, P], F32, name="rt", bufs=1)
             for j in range(2):
-                nc.tensor.transpose(rt[:, j, :], rec[s][:, j : j + 1].to_broadcast([P, P]), ident_f[:])
+                nc.tensor.matmul(
+                    out=rt[:, j, :],
+                    lhsT=rec[s][:, j : j + 1].to_broadcast([P, P]),
+                    rhs=ident_f[:],
+                    start=True,
+                    stop=True,
+                )
             rt_ps[s] = rt
 
         def rt_copy(s):

@@ -111,7 +111,7 @@ def tile_spatialgather_module_t_kernel(tc, feats, probs, out):
             for j in range(2):
                 xw = x_sb[s][:, j, :].bitcast(F32)
                 for g in range(2):
-                    xt = psum.tile([P, 4, P], F32, name="xt", bufs=4)
+                    xt = psum.tile([P, 4, P], F32, name="xt", tag="ring", bufs=6)
                     for h in range(2):
                         for u in range(2):
                             w0 = 512 * h + 256 * g + 128 * u
@@ -130,10 +130,17 @@ def tile_spatialgather_module_t_kernel(tc, feats, probs, out):
                 else:
                     nc.vector.tensor_copy(out=gw[:, j, g], in_=src)
 
-        def qe(s):
+        def qe(s, split):
             eq[s] = qpool.tile([P, N // 2], U32, name="eq", align_bytes=64)
             es[s] = qpool.tile([P, N // 2], U8, name="es", align_bytes=64)
-            nc.vector.quantize_mx(out=eq[s][:].bitcast(FP8X4), scales=es[s][:], in_=ge[s][:])
+            parts = 2 if split else 1
+            w = (N // 2) // parts
+            for i in range(parts):
+                nc.vector.quantize_mx(
+                    out=eq[s][:, i * w : (i + 1) * w].bitcast(FP8X4),
+                    scales=es[s][:, i * w : (i + 1) * w],
+                    in_=ge[s][:, 4 * i * w : 4 * (i + 1) * w],
+                )
 
         def qx(s):
             xq[s] = qpool.tile([P, N], U32, name="xq", align_bytes=64)
@@ -145,31 +152,25 @@ def tile_spatialgather_module_t_kernel(tc, feats, probs, out):
             nc.vector.reciprocal(out=rec[s][:], in_=rowsum[s][:])
 
         def rt_t(s):
-            rt = psum.tile([P, 2, P], F32, name="rt", bufs=1)
+            rt = psum.tile([P, 2, P], F32, name="rt", tag="ring", bufs=6)
             for j in range(2):
-                nc.tensor.matmul(
-                    out=rt[:, j, :],
-                    lhsT=rec[s][:, j : j + 1].to_broadcast([P, P]),
-                    rhs=ident_f[:],
-                    start=True,
-                    stop=True,
-                )
+                nc.tensor.transpose(rt[:, j, :], rec[s][:, j : j + 1].to_broadcast([P, P]), ident_f[:])
             rt_ps[s] = rt
 
         def rt_copy(s):
             rinv[s] = opool.tile([P, 2, P], F32, name="rinv")
             nc.scalar.copy(out=rinv[s][:], in_=rt_ps[s][:])
 
-        def mm(s):
-            acc = psum.tile([P, 4 * P], F32, name="acc", bufs=1)
-            ctx_ps[s] = acc
-            for j in range(2):
+        def mm(s, images):
+            acc = psum.tile([P, len(images), 2, P], F32, name="acc", tag="ring", bufs=6)
+            for i, j in enumerate(images):
+                ctx_ps[(s, j)] = acc
                 for h in range(2):
                     for g in range(2):
                         xo = ((j * 2 + g) * 2 + h) * P
                         eo = (j * 2 + g) * P
                         nc.tensor.matmul_mx(
-                            out=acc[:, (j * 2 + h) * P : (j * 2 + h + 1) * P],
+                            out=acc[:, i, h, :],
                             lhsT=xq[s][:, xo : xo + P].bitcast(FP8X4),
                             lhsT_scale=xs[s][:, xo : xo + P],
                             rhs=eq[s][:, eo : eo + P].bitcast(FP8X4),
@@ -178,17 +179,19 @@ def tile_spatialgather_module_t_kernel(tc, feats, probs, out):
                             stop=(g == 1),
                         )
 
-        def fin(s):
-            o = opool.tile([P, 2, 2, P], F32, name="o_sb")
+        def fin(s, images):
+            n = len(images)
+            j0 = images[0]
+            o = opool.tile([P, n, 2, P], F32, name="o_sb%d" % n)
             nc.vector.tensor_tensor(
                 out=o[:],
-                in0=ctx_ps[s][:].rearrange("p (i h k) -> p i h k", i=2, h=2),
-                in1=rinv[s][:].unsqueeze(2).to_broadcast([P, 2, 2, P]),
+                in0=ctx_ps[(s, j0)][:],
+                in1=rinv[s][:, j0 : j0 + n, :].unsqueeze(2).to_broadcast([P, n, 2, P]),
                 op=ALU.mult,
             )
             queue = nc.sync if s >= NP - 4 else nc.gpsimd
             queue.dma_start(
-                out=out[2 * s : 2 * s + 2].rearrange("b (p h) k o -> p b (h k o)", h=2),
+                out=out[2 * s + j0 : 2 * s + j0 + n].rearrange("b (p h) k o -> p b (h k o)", h=2),
                 in_=o[:].rearrange("p i h k -> p i (h k)"),
             )
 
@@ -202,7 +205,8 @@ def tile_spatialgather_module_t_kernel(tc, feats, probs, out):
         for s in range(LOOK):
             load_l(s)
             load_x(s)
-        for s in range(-4, NP + 1):
+        for s in range(-4, NP):
+            last = s == NP - 1
             if ok(s + 4 + LOOK):
                 load_l(s + 4 + LOOK)
                 load_x(s + 4 + LOOK)
@@ -215,9 +219,9 @@ def tile_spatialgather_module_t_kernel(tc, feats, probs, out):
             if ok(s):
                 rt_t(s)
             if ok(s - 1):
-                mm(s - 1)
-            if ok(s):
-                qe(s)
+                mm(s - 1, [0, 1])
+            if ok(s) and not last:
+                qe(s, False)
             if ok(s + DX):
                 cx(s + DX, range(0, N_SCALAR_BANKS), True)
             if ok(s + 1):
@@ -232,5 +236,12 @@ def tile_spatialgather_module_t_kernel(tc, feats, probs, out):
                 qx(s + DX)
             if ok(s):
                 rt_copy(s)
+            if last:
+                qe(s, True)
             if ok(s - 1):
-                fin(s - 1)
+                fin(s - 1, [0, 1])
+            if last:
+                mm(s, [0])
+                mm(s, [1])
+                fin(s, [0])
+                fin(s, [1])

@@ -159,7 +159,7 @@ def tile_spatialgather_module_t_kernel(tc, feats, probs, out):
 
         def rt_copy(s):
             rinv[s] = opool.tile([P, 2, P], F32, name="rinv")
-            nc.scalar.copy(out=rinv[s][:], in_=rt_ps[s][:])
+            nc.vector.tensor_copy(out=rinv[s][:], in_=rt_ps[s][:])
 
         def mm(s, images):
             acc = psum.tile([P, len(images), 2, P], F32, name="acc", tag="ring", bufs=6)

@@ -159,7 +159,7 @@ def tile_spatialgather_module_t_kernel(tc, feats, probs, out):
 
         def rt_copy(s):
             rinv[s] = opool.tile([P, 2, P], F32, name="rinv")
-            nc.vector.tensor_copy(out=rinv[s][:], in_=rt_ps[s][:])
+            nc.scalar.copy(out=rinv[s][:], in_=rt_ps[s][:])
 
         def mm(s, images):
             acc = psum.tile([P, len(images), 2, P], F32, name="acc", tag="ring", bufs=6)
@@ -222,12 +222,13 @@ def tile_spatialgather_module_t_kernel(tc, feats, probs, out):
                 mm(s - 1, [0, 1])
             if ok(s) and not last:
                 qe(s, False)
+            n_sc = 3 if s + 3 >= NP else (2 if s % 4 == 0 else 1)
             if ok(s + DX):
-                cx(s + DX, range(0, N_SCALAR_BANKS), True)
+                cx(s + DX, range(0, n_sc), True)
             if ok(s + 1):
                 ce(s + 1)
             if ok(s + DX):
-                cx(s + DX, range(N_SCALAR_BANKS, 4), False)
+                cx(s + DX, range(n_sc, 4), False)
             if ok(s + 4):
                 row_max(s + 4)
             if ok(s + 3):

@@ -222,7 +222,7 @@ def tile_spatialgather_module_t_kernel(tc, feats, probs, out):
                 mm(s - 1, [0, 1])
             if ok(s) and not last:
                 qe(s, False)
-            n_sc = 3 if s + 3 >= NP else (2 if s % 4 == 0 else 1)
+            n_sc = 2 if s % 8 == 2 else 1
             if ok(s + DX):
                 cx(s + DX, range(0, n_sc), True)
             if ok(s + 1):

@@ -39,8 +39,6 @@ def tile_spatialgather_module_t_kernel(tc, feats, probs, out):
         opool = ctx.enter_context(tc.tile_pool(name="opool", bufs=3))
         psum = ctx.enter_context(tc.psum_pool(name="psum", bufs=1))
 
-        ident_bf = const.tile([P, P], BF16, name="ident_bf")
-        make_identity(nc, ident_bf[:])
         ident_f = const.tile([P, P], F32, name="ident_f")
         make_identity(nc, ident_f[:])
 
@@ -80,8 +78,8 @@ def tile_spatialgather_module_t_kernel(tc, feats, probs, out):
             for j in range(2):
                 e = epool.tile([P, N], BF16, name="e_sb")
                 nc.scalar.activation(
-                    out=e[:].rearrange("k (a e p) -> k a e p", a=4, e=2),
-                    in_=l_sb[s][:, j, :].rearrange("k (a p e) -> k a e p", a=4, e=2),
+                    out=e[:],
+                    in_=l_sb[s][:, j, :],
                     func=ACT.Exp,
                     bias=negmax[s][:, j : j + 1],
                     scale=1.0,
@@ -93,17 +91,18 @@ def tile_spatialgather_module_t_kernel(tc, feats, probs, out):
 
         def te(s):
             for j in range(2):
-                et = psum.tile([P, 8, P], BF16, name="et", bufs=2)
-                for ch in range(8):
-                    nc.tensor.transpose(et[:, ch, :], e_sb[(s, j)][:, ch * P : (ch + 1) * P], ident_bf[:])
+                ew = e_sb[(s, j)][:].bitcast(F32)
+                et = psum.tile([P, 4, P], F32, name="et", bufs=2)
+                for ch in range(4):
+                    nc.tensor.transpose(et[:, ch, :], ew[:, ch * P : (ch + 1) * P], ident_f[:])
                 et_ps[(s, j)] = et
 
         def ce(s):
             g = gpool.tile([P, 2 * N], BF16, name="ge", align_bytes=64)
             ge[s] = g
-            gv = g[:].rearrange("p (i g k t) -> p i g k t", i=2, g=2, t=4)
+            gv = g[:].bitcast(F32).rearrange("p (i g k u) -> p i g k u", i=2, g=2, u=2)
             for j in range(2):
-                nc.scalar.copy(out=gv[:, j], in_=et_ps[(s, j)][:].rearrange("p (g t) k -> p g k t", t=4))
+                nc.scalar.copy(out=gv[:, j], in_=et_ps[(s, j)][:].rearrange("p (g u) k -> p g k u", u=2))
 
         xt_ps = {}
 
@@ -222,7 +221,7 @@ def tile_spatialgather_module_t_kernel(tc, feats, probs, out):
                 mm(s - 1, [0, 1])
             if ok(s) and not last:
                 qe(s, False)
-            n_sc = 2 if s % 8 == 2 else 1
+            n_sc = 2
             if ok(s + DX):
                 cx(s + DX, range(0, n_sc), True)
             if ok(s + 1):

@@ -36,7 +36,7 @@ def tile_spatialgather_module_t_kernel(tc, feats, probs, out):
         epool = ctx.enter_context(tc.tile_pool(name="epool", bufs=8))
         gpool = ctx.enter_context(tc.tile_pool(name="gpool", bufs=3))
         qpool = ctx.enter_context(tc.tile_pool(name="qpool", bufs=DX + 3))
-        opool = ctx.enter_context(tc.tile_pool(name="opool", bufs=3))
+        opool = ctx.enter_context(tc.tile_pool(name="opool", bufs=8))
         psum = ctx.enter_context(tc.psum_pool(name="psum", bufs=1))
 
         ident_f = const.tile([P, P], F32, name="ident_f")
@@ -188,8 +188,7 @@ def tile_spatialgather_module_t_kernel(tc, feats, probs, out):
                 in1=rinv[s][:, j0 : j0 + n, :].unsqueeze(2).to_broadcast([P, n, 2, P]),
                 op=ALU.mult,
             )
-            queue = nc.sync if s >= NP - 4 else nc.gpsimd
-            queue.dma_start(
+            nc.sync.dma_start(
                 out=out[2 * s + j0 : 2 * s + j0 + n].rearrange("b (p h) k o -> p b (h k o)", h=2),
                 in_=o[:].rearrange("p i h k -> p i (h k)"),
             )
@@ -209,8 +208,6 @@ def tile_spatialgather_module_t_kernel(tc, feats, probs, out):
             if ok(s + 4 + LOOK):
                 load_l(s + 4 + LOOK)
                 load_x(s + 4 + LOOK)
-            if ok(s):
-                recip(s)
             if ok(s + 1):
                 te(s + 1)
             if ok(s + DX):
@@ -232,6 +229,8 @@ def tile_spatialgather_module_t_kernel(tc, feats, probs, out):
                 row_max(s + 4)
             if ok(s + 3):
                 exps(s + 3)
+            if ok(s + 2):
+                recip(s + 2)
             if ok(s + DX):
                 qx(s + DX)
             if ok(s):

@@ -42,6 +42,11 @@ def tile_spatialgather_module_t_kernel(tc, feats, probs, out):
         ident_f = const.tile([P, P], F32, name="ident_f")
         make_identity(nc, ident_f[:])
 
+        warm = const.tile([P, 1], F32, name="warm")
+        nc.vector.memset(warm[:], 0.0)
+        warm_exp = const.tile([P, 1], F32, name="warm_exp")
+        nc.scalar.activation(out=warm_exp[:], in_=warm[:], func=ACT.Exp)
+
         l_sb, x_sb, negmax, rowsum, e_sb = {}, {}, {}, {}, {}
         ge, gx, eq, es, xq, xs, rinv, rec, rt_ps, ctx_ps = {}, {}, {}, {}, {}, {}, {}, {}, {}, {}
 

@@ -80,7 +80,7 @@ def tile_spatialgather_module_t_kernel(tc, feats, probs, out):
         def exps(s):
             rs = small.tile([P, 2], F32, name="rs")
             rowsum[s] = rs
-            for j in range(2):
+            for j in (0, 1) if s == 0 else (1, 0):
                 e = epool.tile([P, N], BF16, name="e_sb")
                 nc.scalar.activation(
                     out=e[:],
@@ -106,7 +106,7 @@ def tile_spatialgather_module_t_kernel(tc, feats, probs, out):
             g = gpool.tile([P, 2 * N], BF16, name="ge", align_bytes=64)
             ge[s] = g
             gv = g[:].bitcast(F32).rearrange("p (i g k u) -> p i g k u", i=2, g=2, u=2)
-            for j in range(2):
+            for j in (1, 0):
                 nc.scalar.copy(out=gv[:, j], in_=et_ps[(s, j)][:].rearrange("p (g u) k -> p g k u", u=2))
 
         xt_ps = {}
@@ -126,7 +126,7 @@ def tile_spatialgather_module_t_kernel(tc, feats, probs, out):
             if s not in gx:
                 gx[s] = gpool.tile([P, 4 * N], BF16, name="gx", align_bytes=64)
             gw = gx[s][:].bitcast(F32).rearrange("p (i g h c u) -> p i g h c u", i=2, g=2, h=2, u=2)
-            for b in banks:
+            for b in reversed(banks):
                 j, g = b // 2, b % 2
                 src = xt_ps[(s, j, g)][:].rearrange("p (h u) c -> p h c u", u=2)
                 if on_scalar:

@@ -193,7 +193,8 @@ def tile_spatialgather_module_t_kernel(tc, feats, probs, out):
                 in1=rinv[s][:, j0 : j0 + n, :].unsqueeze(2).to_broadcast([P, n, 2, P]),
                 op=ALU.mult,
             )
-            nc.sync.dma_start(
+            queue = nc.sync if s >= NP - 4 else nc.gpsimd
+            queue.dma_start(
                 out=out[2 * s + j0 : 2 * s + j0 + n].rearrange("b (p h) k o -> p b (h k o)", h=2),
                 in_=o[:].rearrange("p i h k -> p i (h k)"),
             )

from contextlib import ExitStack

import concourse.mybir as mybir
from concourse.masks import make_identity

BF16 = mybir.dt.bfloat16
F32 = mybir.dt.float32
U32 = mybir.dt.uint32
U8 = mybir.dt.uint8
FP8X4 = mybir.dt.float8_e4m3fn_x4
ACT = mybir.ActivationFunctionType
ALU = mybir.AluOpType
AX = mybir.AxisListType

B = 32
C = 256
K = 128
N = 1024
P = 128
NP = B // 2
FLOPS = 2 * B * K * C * N

PIN = True
DX = 2
N_SCALAR_BANKS = 1


def tile_spatialgather_module_t_kernel(tc, feats, probs, out):
    nc = tc.nc
    with ExitStack() as ctx:
        const = ctx.enter_context(tc.tile_pool(name="const", bufs=1))
        lpool = ctx.enter_context(tc.tile_pool(name="lpool", bufs=8))
        xpool = ctx.enter_context(tc.tile_pool(name="xpool", bufs=8))
        tree = ctx.enter_context(tc.tile_pool(name="tree", bufs=2))
        small = ctx.enter_context(tc.tile_pool(name="small", bufs=8))
        epool = ctx.enter_context(tc.tile_pool(name="epool", bufs=8))
        gpool = ctx.enter_context(tc.tile_pool(name="gpool", bufs=3))
        qpool = ctx.enter_context(tc.tile_pool(name="qpool", bufs=DX + 3))
        opool = ctx.enter_context(tc.tile_pool(name="opool", bufs=8))
        psum = ctx.enter_context(tc.psum_pool(name="psum", bufs=1))

        ident_f = const.tile([P, P], F32, name="ident_f")
        make_identity(nc, ident_f[:])

        warm = const.tile([P, 1], F32, name="warm")
        nc.vector.memset(warm[:], 0.0)
        warm_exp = const.tile([P, 1], F32, name="warm_exp")
        nc.scalar.activation(out=warm_exp[:], in_=warm[:], func=ACT.Exp)

        l_sb, x_sb, negmax, rowsum, e_sb = {}, {}, {}, {}, {}
        ge, gx, eq, es, xq, xs, rinv, rec, rt_ps, ctx_ps = {}, {}, {}, {}, {}, {}, {}, {}, {}, {}

        def load_l(s):
            t = lpool.tile([P, 2, N], BF16, name="l_sb")
            nc.sync.dma_start(out=t[:], in_=probs[2 * s : 2 * s + 2].rearrange("b k y x -> k b (y x)"))
            l_sb[s] = t

        def load_x(s):
            t = xpool.tile([P, 2, 2 * N], BF16, name="x_sb")
            nc.sync.dma_start(
                out=t[:], in_=feats[2 * s : 2 * s + 2].rearrange("b (p h) y x -> p b (h y x)", h=2)
            )
            x_sb[s] = t

        def row_max(s):
            nm = small.tile([P, 2], F32, name="nm")
            for j in range(2):
                junk = tree.tile([P, N], BF16, name="junk")
                nc.vector.tensor_scalar(
                    out=junk[:],
                    in0=l_sb[s][:, j, :],
                    scalar1=-1.0,
                    scalar2=None,
                    op0=ALU.mult,
                    op1=ALU.min,
                    accum_out=nm[:, j : j + 1],
                )
            negmax[s] = nm

        def exps(s):
            rs = small.tile([P, 2], F32, name="rs")
            rowsum[s] = rs
            for j in (0, 1) if s == 0 else (1, 0):
                e = epool.tile([P, N], BF16, name="e_sb")
                nc.scalar.activation(
                    out=e[:],
                    in_=l_sb[s][:, j, :],
                    func=ACT.Exp,
                    bias=negmax[s][:, j : j + 1],
                    scale=1.0,
                    accum_out=rs[:, j : j + 1],
                )
                e_sb[(s, j)] = e

        et_ps = {}

        def te(s):
            for j in range(2):
                ew = e_sb[(s, j)][:].bitcast(F32)
                et = psum.tile([P, 4, P], F32, name="et", bufs=2)
                for ch in range(4):
                    nc.tensor.transpose(et[:, ch, :], ew[:, ch * P : (ch + 1) * P], ident_f[:])
                et_ps[(s, j)] = et

        def ce(s):
            g = gpool.tile([P, 2 * N], BF16, name="ge", align_bytes=64)
            ge[s] = g
            gv = g[:].bitcast(F32).rearrange("p (i g k u) -> p i g k u", i=2, g=2, u=2)
            for j in (1, 0):
                nc.scalar.copy(out=gv[:, j], in_=et_ps[(s, j)][:].rearrange("p (g u) k -> p g k u", u=2))

        xt_ps = {}

        def tx(s):
            for j in range(2):
                xw = x_sb[s][:, j, :].bitcast(F32)
                for g in range(2):
                    xt = psum.tile([P, 4, P], F32, name="xt", tag="ring", bufs=6)
                    for h in range(2):
                        for u in range(2):
                            w0 = 512 * h + 256 * g + 128 * u
                            nc.tensor.transpose(xt[:, 2 * h + u, :], xw[:, w0 : w0 + P], ident_f[:])
                    xt_ps[(s, j, g)] = xt

        def cx(s, banks, on_scalar):
            if s not in gx:
                gx[s] = gpool.tile([P, 4 * N], BF16, name="gx", align_bytes=64)
            gw = gx[s][:].bitcast(F32).rearrange("p (i g h c u) -> p i g h c u", i=2, g=2, h=2, u=2)
            for b in reversed(banks):
                j, g = b // 2, b % 2
                src = xt_ps[(s, j, g)][:].rearrange("p (h u) c -> p h c u", u=2)
                if on_scalar:
                    nc.scalar.copy(out=gw[:, j, g], in_=src)
                else:
                    nc.vector.tensor_copy(out=gw[:, j, g], in_=src)

        def qe(s, split):
            eq[s] = qpool.tile([P, N // 2], U32, name="eq", align_bytes=64)
            es[s] = qpool.tile([P, N // 2], U8, name="es", align_bytes=64)
            parts = 2 if split else 1
            w = (N // 2) // parts
            for i in range(parts):
                nc.vector.quantize_mx(
                    out=eq[s][:, i * w : (i + 1) * w].bitcast(FP8X4),
                    scales=es[s][:, i * w : (i + 1) * w],
                    in_=ge[s][:, 4 * i * w : 4 * (i + 1) * w],
                )

        def qx(s):
            xq[s] = qpool.tile([P, N], U32, name="xq", align_bytes=64)
            xs[s] = qpool.tile([P, N], U8, name="xs", align_bytes=64)
            nc.vector.quantize_mx(out=xq[s][:].bitcast(FP8X4), scales=xs[s][:], in_=gx[s][:])

        def recip(s):
            rec[s] = small.tile([P, 2], F32, name="rec")
            nc.vector.reciprocal(out=rec[s][:], in_=rowsum[s][:])

        def rt_t(s):
            rt = psum.tile([P, 2, P], F32, name="rt", tag="ring", bufs=6)
            for j in range(2):
                nc.tensor.transpose(rt[:, j, :], rec[s][:, j : j + 1].to_broadcast([P, P]), ident_f[:])
            rt_ps[s] = rt

        def rt_copy(s):
            rinv[s] = opool.tile([P, 2, P], F32, name="rinv")
            nc.scalar.copy(out=rinv[s][:], in_=rt_ps[s][:])

        def mm(s, images):
            acc = psum.tile([P, len(images), 2, P], F32, name="acc", tag="ring", bufs=6)
            for i, j in enumerate(images):
                ctx_ps[(s, j)] = acc
                for h in range(2):
                    for g in range(2):
                        xo = ((j * 2 + g) * 2 + h) * P
                        eo = (j * 2 + g) * P
                        nc.tensor.matmul_mx(
                            out=acc[:, i, h, :],
                            lhsT=xq[s][:, xo : xo + P].bitcast(FP8X4),
                            lhsT_scale=xs[s][:, xo : xo + P],
                            rhs=eq[s][:, eo : eo + P].bitcast(FP8X4),
                            rhs_scale=es[s][:, eo : eo + P],
                            start=(g == 0),
                            stop=(g == 1),
                        )

        def fin(s, images):
            n = len(images)
            j0 = images[0]
            o = opool.tile([P, n, 2, P], F32, name="o_sb%d" % n)
            nc.vector.tensor_tensor(
                out=o[:],
                in0=ctx_ps[(s, j0)][:],
                in1=rinv[s][:, j0 : j0 + n, :].unsqueeze(2).to_broadcast([P, n, 2, P]),
                op=ALU.mult,
            )
            queue = nc.sync if s >= NP - 4 else nc.gpsimd
            queue.dma_start(
                out=out[2 * s + j0 : 2 * s + j0 + n].rearrange("b (p h) k o -> p b (h k o)", h=2),
                in_=o[:].rearrange("p i h k -> p i (h k)"),
            )

        def ok(s):
            return 0 <= s < NP

        if PIN:
            ctx.enter_context(tc.manual_schedule())

        LOOK = 5
        for s in range(LOOK):
            load_l(s)
            load_x(s)
        for s in range(-4, NP):
            last = s == NP - 1
            if ok(s + 4 + LOOK):
                load_l(s + 4 + LOOK)
                load_x(s + 4 + LOOK)
            if ok(s + 1):
                te(s + 1)
            if ok(s + DX):
                tx(s + DX)
            if ok(s):
                rt_t(s)
            if ok(s - 1):
                mm(s - 1, [0, 1])
            if ok(s) and not last:
                qe(s, False)
            n_sc = 2
            if ok(s + DX):
                cx(s + DX, range(0, n_sc), True)
            if ok(s + 1):
                ce(s + 1)
            if ok(s + DX):
                cx(s + DX, range(n_sc, 4), False)
            if ok(s + 4):
                row_max(s + 4)
            if ok(s + 3):
                exps(s + 3)
            if ok(s + 2):
                recip(s + 2)
            if ok(s + DX):
                qx(s + DX)
            if ok(s):
                rt_copy(s)
            if last:
                qe(s, True)
            if ok(s - 1):
                fin(s - 1, [0, 1])
            if last:
                mm(s, [0])
                mm(s, [1])
                fin(s, [0])
                fin(s, [1])
